import numpy as np
import ml_dtypes

BF16 = ml_dtypes.bfloat16


def bf(x):
    return np.asarray(x, np.float32).astype(BF16)


def f32(x):
    return np.asarray(x, np.float32)


def f64(x):
    return np.asarray(x).astype(np.float64)


def striped(idx):
    return np.tile(idx.reshape(-1, 16).T, (8, 1))


C, S, N, HD = 128, 1024, 128, 8


def sigmoid(v):
    return 1.0 / (1.0 + np.exp(-v))


def setup_inputs():
    x = bf(np.random.standard_normal((C, N)))
    wq = bf(np.random.standard_normal((C, C)) / np.sqrt(C))
    wr = bf(np.repeat(np.random.standard_normal((C, C // HD)) / np.sqrt(C), HD, axis=1))
    br = f32(np.repeat(0.5 * np.random.standard_normal((C // HD, 1)), HD, axis=0))
    base = f32(np.random.standard_normal((C, S)))
    return {"x": x, "wq": wq, "wr": wr, "br": br, "base": base, "offs": striped(np.random.permutation(S)[:N])}


def reference(x, wq, wr, br, base, offs):
    idx = offs[:16].T.reshape(-1)
    q = f64(wq).T @ f64(x)
    gate = sigmoid(f64(wr).T @ f64(x) + f64(br))
    out = f64(base).copy()
    out[:, idx] = q * gate
    return out

@@ -1,0 +1,50 @@
+import concourse.mybir as mybir
+
+CHANNELS = 128
+FEATURES = 128
+TOKENS = 128
+SLOTS = 1024
+
+FLOPS = 2 * 2 * FEATURES * CHANNELS * TOKENS
+
+F32 = mybir.dt.float32
+BF16 = mybir.dt.bfloat16
+U16 = mybir.dt.uint16
+
+
+def tile_causalselfattention_kernel(tc, x, wq, wr, br, base, offs, out):
+    nc = tc.nc
+    with (
+        tc.tile_pool(name="held", bufs=1) as held,
+        tc.psum_pool(name="psum", bufs=1) as psum,
+    ):
+        offsets = held.tile([CHANNELS, TOKENS // 16], U16, name="offsets")
+        nc.sync.dma_start(offsets[:], offs)
+        window = held.tile([CHANNELS, SLOTS], F32, name="window")
+        nc.sync.dma_start(window[:], base)
+
+        x_sb = held.tile([FEATURES, TOKENS], BF16, name="x_sb")
+        nc.scalar.dma_start(x_sb[:], x)
+        wr_sb = held.tile([FEATURES, CHANNELS], BF16, name="wr_sb")
+        nc.scalar.dma_start(wr_sb[:], wr)
+        br_sb = held.tile([CHANNELS, 1], F32, name="br_sb")
+        nc.scalar.dma_start(br_sb[:], br)
+        wq_sb = held.tile([FEATURES, CHANNELS], BF16, name="wq_sb")
+        nc.scalar.dma_start(wq_sb[:], wq)
+
+        route_ps = psum.tile([CHANNELS, TOKENS], F32, name="route_ps")
+        nc.tensor.matmul(route_ps[:], wr_sb[:], x_sb[:], start=True, stop=True)
+        query_ps = psum.tile([CHANNELS, TOKENS], F32, name="query_ps")
+        nc.tensor.matmul(query_ps[:], wq_sb[:], x_sb[:], start=True, stop=True)
+
+        gate = held.tile([CHANNELS, TOKENS], F32, name="gate")
+        nc.scalar.activation(
+            gate[:], route_ps[:], mybir.ActivationFunctionType.Sigmoid, bias=br_sb[:, 0:1]
+        )
+        query = held.tile([CHANNELS, TOKENS], F32, name="query")
+        nc.vector.tensor_copy(query[:], query_ps[:])
+
+        nc.vector.tensor_tensor(
+            window[:].indirect(offsets[:]), query[:], gate[:], mybir.AluOpType.mult
+        )
+        nc.sync.dma_start(out, window[:])

@@ -32,6 +32,10 @@ def tile_causalselfattention_kernel(tc, x, wq, wr, br, base, offs, out):
         wq_sb = held.tile([FEATURES, CHANNELS], BF16, name="wq_sb")
         nc.scalar.dma_start(wq_sb[:], wq)
 
+        warm = held.tile([CHANNELS, 1], F32, name="warm")
+        nc.vector.memset(warm[:], 0.0)
+        nc.scalar.activation(warm[:], warm[:], mybir.ActivationFunctionType.Sigmoid)
+
         route_ps = psum.tile([CHANNELS, TOKENS], F32, name="route_ps")
         nc.tensor.matmul(route_ps[:], wr_sb[:], x_sb[:], start=True, stop=True)
         query_ps = psum.tile([CHANNELS, TOKENS], F32, name="query_ps")

@@ -4,6 +4,7 @@ CHANNELS = 128
 FEATURES = 128
 TOKENS = 128
 SLOTS = 1024
+HALF = SLOTS // 2
 
 FLOPS = 2 * 2 * FEATURES * CHANNELS * TOKENS
 
@@ -19,18 +20,19 @@ def tile_causalselfattention_kernel(tc, x, wq, wr, br, base, offs, out):
         tc.psum_pool(name="psum", bufs=1) as psum,
     ):
         offsets = held.tile([CHANNELS, TOKENS // 16], U16, name="offsets")
-        nc.sync.dma_start(offsets[:], offs)
         window = held.tile([CHANNELS, SLOTS], F32, name="window")
-        nc.sync.dma_start(window[:], base)
-
         x_sb = held.tile([FEATURES, TOKENS], BF16, name="x_sb")
-        nc.scalar.dma_start(x_sb[:], x)
         wr_sb = held.tile([FEATURES, CHANNELS], BF16, name="wr_sb")
-        nc.scalar.dma_start(wr_sb[:], wr)
         br_sb = held.tile([CHANNELS, 1], F32, name="br_sb")
-        nc.scalar.dma_start(br_sb[:], br)
         wq_sb = held.tile([FEATURES, CHANNELS], BF16, name="wq_sb")
-        nc.scalar.dma_start(wq_sb[:], wq)
+
+        nc.sync.dma_start(window[:, 0:HALF], base[:, 0:HALF])
+        nc.sync.dma_start(offsets[:], offs)
+        nc.sync.dma_start(wq_sb[:], wq)
+        nc.scalar.dma_start(x_sb[:], x)
+        nc.scalar.dma_start(wr_sb[:], wr)
+        nc.scalar.dma_start(br_sb[:], br)
+        nc.scalar.dma_start(window[:, HALF:SLOTS], base[:, HALF:SLOTS])
 
         warm = held.tile([CHANNELS, 1], F32, name="warm")
         nc.vector.memset(warm[:], 0.0)

@@ -26,13 +26,13 @@ def tile_causalselfattention_kernel(tc, x, wq, wr, br, base, offs, out):
         br_sb = held.tile([CHANNELS, 1], F32, name="br_sb")
         wq_sb = held.tile([FEATURES, CHANNELS], BF16, name="wq_sb")
 
-        nc.sync.dma_start(window[:, 0:HALF], base[:, 0:HALF])
-        nc.sync.dma_start(offsets[:], offs)
-        nc.sync.dma_start(wq_sb[:], wq)
-        nc.scalar.dma_start(x_sb[:], x)
+        nc.sync.dma_start(x_sb[:], x)
         nc.scalar.dma_start(wr_sb[:], wr)
         nc.scalar.dma_start(br_sb[:], br)
+        nc.sync.dma_start(wq_sb[:], wq)
+        nc.sync.dma_start(offsets[:], offs)
         nc.scalar.dma_start(window[:, HALF:SLOTS], base[:, HALF:SLOTS])
+        nc.sync.dma_start(window[:, 0:HALF], base[:, 0:HALF])
 
         warm = held.tile([CHANNELS, 1], F32, name="warm")
         nc.vector.memset(warm[:], 0.0)

@@ -27,12 +27,12 @@ def tile_causalselfattention_kernel(tc, x, wq, wr, br, base, offs, out):
         wq_sb = held.tile([FEATURES, CHANNELS], BF16, name="wq_sb")
 
         nc.sync.dma_start(x_sb[:], x)
-        nc.scalar.dma_start(wr_sb[:], wr)
-        nc.scalar.dma_start(br_sb[:], br)
+        nc.sync.dma_start(wr_sb[:], wr)
+        nc.sync.dma_start(br_sb[:], br)
         nc.sync.dma_start(wq_sb[:], wq)
         nc.sync.dma_start(offsets[:], offs)
-        nc.scalar.dma_start(window[:, HALF:SLOTS], base[:, HALF:SLOTS])
         nc.sync.dma_start(window[:, 0:HALF], base[:, 0:HALF])
+        nc.sync.dma_start(window[:, HALF:SLOTS], base[:, HALF:SLOTS])
 
         warm = held.tile([CHANNELS, 1], F32, name="warm")
         nc.vector.memset(warm[:], 0.0)

@@ -30,8 +30,8 @@ def tile_causalselfattention_kernel(tc, x, wq, wr, br, base, offs, out):
         nc.sync.dma_start(wr_sb[:], wr)
         nc.sync.dma_start(br_sb[:], br)
         nc.sync.dma_start(wq_sb[:], wq)
-        nc.sync.dma_start(offsets[:], offs)
         nc.sync.dma_start(window[:, 0:HALF], base[:, 0:HALF])
+        nc.sync.dma_start(offsets[:], offs)
         nc.sync.dma_start(window[:, HALF:SLOTS], base[:, HALF:SLOTS])
 
         warm = held.tile([CHANNELS, 1], F32, name="warm")
@@ -48,7 +48,7 @@ def tile_causalselfattention_kernel(tc, x, wq, wr, br, base, offs, out):
             gate[:], route_ps[:], mybir.ActivationFunctionType.Sigmoid, bias=br_sb[:, 0:1]
         )
         query = held.tile([CHANNELS, TOKENS], F32, name="query")
-        nc.vector.tensor_copy(query[:], query_ps[:])
+        nc.scalar.copy(query[:], query_ps[:])
 
         nc.vector.tensor_tensor(
             window[:].indirect(offsets[:]), query[:], gate[:], mybir.AluOpType.mult

import concourse.mybir as mybir

CHANNELS = 128
FEATURES = 128
TOKENS = 128
SLOTS = 1024
HALF = SLOTS // 2

FLOPS = 2 * 2 * FEATURES * CHANNELS * TOKENS

F32 = mybir.dt.float32
BF16 = mybir.dt.bfloat16
U16 = mybir.dt.uint16


def tile_causalselfattention_kernel(tc, x, wq, wr, br, base, offs, out):
    nc = tc.nc
    with (
        tc.tile_pool(name="held", bufs=1) as held,
        tc.psum_pool(name="psum", bufs=1) as psum,
    ):
        offsets = held.tile([CHANNELS, TOKENS // 16], U16, name="offsets")
        window = held.tile([CHANNELS, SLOTS], F32, name="window")
        x_sb = held.tile([FEATURES, TOKENS], BF16, name="x_sb")
        wr_sb = held.tile([FEATURES, CHANNELS], BF16, name="wr_sb")
        br_sb = held.tile([CHANNELS, 1], F32, name="br_sb")
        wq_sb = held.tile([FEATURES, CHANNELS], BF16, name="wq_sb")

        nc.sync.dma_start(x_sb[:], x)
        nc.sync.dma_start(wr_sb[:], wr)
        nc.sync.dma_start(br_sb[:], br)
        nc.sync.dma_start(wq_sb[:], wq)
        nc.sync.dma_start(window[:, 0:HALF], base[:, 0:HALF])
        nc.sync.dma_start(offsets[:], offs)
        nc.sync.dma_start(window[:, HALF:SLOTS], base[:, HALF:SLOTS])

        warm = held.tile([CHANNELS, 1], F32, name="warm")
        nc.vector.memset(warm[:], 0.0)
        nc.scalar.activation(warm[:], warm[:], mybir.ActivationFunctionType.Sigmoid)

        route_ps = psum.tile([CHANNELS, TOKENS], F32, name="route_ps")
        nc.tensor.matmul(route_ps[:], wr_sb[:], x_sb[:], start=True, stop=True)
        query_ps = psum.tile([CHANNELS, TOKENS], F32, name="query_ps")
        nc.tensor.matmul(query_ps[:], wq_sb[:], x_sb[:], start=True, stop=True)

        gate = held.tile([CHANNELS, TOKENS], F32, name="gate")
        nc.scalar.activation(
            gate[:], route_ps[:], mybir.ActivationFunctionType.Sigmoid, bias=br_sb[:, 0:1]
        )
        query = held.tile([CHANNELS, TOKENS], F32, name="query")
        nc.scalar.copy(query[:], query_ps[:])

        nc.vector.tensor_tensor(
            window[:].indirect(offsets[:]), query[:], gate[:], mybir.AluOpType.mult
        )
        nc.sync.dma_start(out, window[:])
